import numpy as np
import ml_dtypes


def mxq(x, axis, fmt="e4m3"):
    dtype, down = {"e4m3": (ml_dtypes.float8_e4m3fn, 7), "e5m2": (ml_dtypes.float8_e5m2, 14)}[fmt]
    v = np.moveaxis(np.asarray(x, np.float32).astype(ml_dtypes.bfloat16).astype(np.float64), axis, -1)
    blocks = v.reshape(v.shape[:-1] + (-1, 32))
    amax = np.abs(blocks).max(-1, keepdims=True)
    byte = np.maximum(np.where(amax > 0, np.frexp(amax)[1] - 1 + 127, 0) - down, 1)
    scale = np.exp2(byte - 127.0)
    codes = (blocks / scale).astype(np.float32).astype(dtype).astype(np.float64)
    return np.moveaxis((codes * scale).reshape(v.shape), -1, axis)


WIDE = False


def mx_kscale(k):
    if not WIDE:
        return np.ones(k)
    levels = np.array([10, -10, 5, -5, 0])
    if k % 512:
        return np.exp2(np.random.permutation(np.resize(levels, k // 32))).repeat(32)
    a = np.empty((k // 512, 16))
    for p in range(k // 512):
        a[p, :8] = np.random.permutation(np.resize(levels, 8))
        for g in range(8):
            far = levels[np.abs(levels - a[p, g]) >= 10]
            a[p, g + 8] = far[np.random.randint(len(far))]
    return np.exp2(a.ravel()).repeat(32)


BF16 = ml_dtypes.bfloat16


def bf(x):
    return np.asarray(x, np.float32).astype(BF16)


def f64(x):
    return np.asarray(x).astype(np.float64)


B, F, H, C = 1024, 1024, 512, 10
EPS = 4.0 / 30.0
P_KEEP = 0.95


def setup_inputs():
    s = mx_kscale(F)
    ns = EPS / (6.0 * np.sqrt(H))
    return {"x1": bf(np.random.standard_normal((B, F)) * s),
            "x2": bf(np.random.standard_normal((B, F)) * s),
            "W1": bf(np.random.standard_normal((F, H)) / np.sqrt(F) / s[:, None]),
            "b1": bf(np.random.standard_normal(H) * 0.3),
            "W2": bf(np.random.standard_normal((F, H)) / np.sqrt(F) / s[:, None]),
            "b2": bf(np.random.standard_normal(H) * 0.3),
            "noise_std": bf(np.random.laplace(size=(B, H)) * ns),
            "rr_uniform": bf(np.random.uniform(size=H))}


def core(x1, x2, W1, b1, W2, b2, noise_std, rr_uniform):
    out1 = (mxq(f64(x1), 1, "e4m3") @ mxq(f64(W1), 0, "e4m3")) + f64(b1)
    one_norm = np.sum(np.abs(out1), axis=1)
    sensitivity = np.max(one_norm) - np.min(one_norm)
    noise_mul = sensitivity / EPS
    out1 = out1 + f64(noise_std) * noise_mul
    rr_mask = np.where(f64(rr_uniform) < P_KEEP, 1.0, 0.0)
    out1 = out1 * rr_mask
    out2 = (mxq(f64(x2), 1, "e4m3") @ mxq(f64(W2), 0, "e4m3")) + f64(b2)
    return np.minimum(out1, out2)


def e4m3fn_bytes(y):
    return np.clip(np.asarray(y, np.float64), -448.0, 448.0).astype(np.float32).astype(ml_dtypes.float8_e4m3fn).view(np.uint8)


def reference(x1, x2, W1, b1, W2, b2, noise_std, rr_uniform):
    out = core(x1, x2, W1, b1, W2, b2, noise_std, rr_uniform)
    s = np.max(np.abs(out), axis=-1, keepdims=True) / 448.0
    return out, e4m3fn_bytes(out / s)

@@ -1,0 +1,368 @@
+from contextlib import ExitStack
+
+import concourse.mybir as mybir
+from concourse.masks import make_identity
+
+F32 = mybir.dt.float32
+BF16 = mybir.dt.bfloat16
+U32 = mybir.dt.uint32
+U8 = mybir.dt.uint8
+FP8X4 = mybir.dt.float8_e4m3fn_x4
+FP8 = mybir.dt.float8_e4m3fn
+ALU = mybir.AluOpType
+ACT = mybir.ActivationFunctionType
+AX = mybir.AxisListType
+
+B, F, H = 1024, 1024, 512
+EPS = 4.0 / 30.0
+P_KEEP = 0.95
+FP8_MAX = 448.0
+FLOPS = 2 * 2 * B * F * H
+
+P = 128
+PACK = 4
+K_PASS = P * PACK
+N_PASS = F // K_PASS
+N_TILE = B // P
+N_PAIR = N_TILE // 2
+N_HALF = 2
+TILES_PER_HALF = N_TILE // N_HALF
+N_CH = H // P
+PSUM_BANKS = 8
+
+W1_VECTOR_COLS = 352
+W2_PIECE_COLS = 128
+VECTOR_CASTS = (3, 5, 7)
+
+
+def tile_splitnn_pa_kernel(tc, x1, x2, W1, b1, W2, b2, noise_std, rr_uniform, out_0, out_1):
+    nc = tc.nc
+
+    with ExitStack() as ctx:
+        sb = ctx.enter_context(tc.tile_pool(name="sb", bufs=1))
+        scratch = ctx.enter_context(tc.tile_pool(name="scratch", bufs=2))
+        ps = ctx.enter_context(tc.psum_pool(name="ps", bufs=PSUM_BANKS))
+        ctx.enter_context(tc.manual_schedule())
+
+        banks = {}
+
+        def new_bank(key, shape, dtype):
+            banks[key] = ps.tile(shape, dtype, name="bank")
+            return banks[key]
+
+        zero_col = sb.tile([P, 1], F32, name="zero_col")
+        act_warm = sb.tile([P, 1], F32, name="act_warm")
+        ones = sb.tile([P, P], BF16, name="ones")
+        ident_f32 = sb.tile([P, P], F32, name="ident_f32")
+        ident_bf16 = sb.tile([P, P], BF16, name="ident_bf16")
+        b1_row = sb.tile([P, H], BF16, name="b1_row")
+        vec_rows = sb.tile([P, P], BF16, name="vec_rows")
+        b1_all = sb.tile([P, H], F32, name="b1_all")
+        vec_cols = sb.tile([P, 2 * N_CH], F32, name="vec_cols")
+        keep_cols = sb.tile([P, N_CH], F32, name="keep_cols")
+        norms = sb.tile([P, 2, N_TILE], F32, name="norms")
+        part_ext = sb.tile([P, 2], F32, name="part_ext")
+        all_ext = sb.tile([P, 2], F32, name="all_ext")
+        noise_mul = sb.tile([P, 1], F32, name="noise_mul")
+        row_amax = sb.tile([P, N_TILE], F32, name="row_amax")
+        row_rcp = sb.tile([P, N_TILE], F32, name="row_rcp")
+        row_scale = sb.tile([P, N_TILE], F32, name="row_scale")
+
+        x_raw = [[sb.tile([P, 2, F], BF16, name="x_raw%d_%d" % (c, k)) for k in range(N_PAIR)] for c in range(2)]
+        w_raw = [[sb.tile([P, PACK, H], BF16, name="w_raw%d_%d" % (c, s)) for s in range(N_PASS)] for c in range(2)]
+        noise = sb.tile([P, N_TILE, H], BF16, name="noise")
+
+        w_grouped = [sb.tile([P, N_PASS, H, PACK], BF16, name="w_grouped%d" % c, align_bytes=64) for c in range(2)]
+        w_codes = [sb.tile([P, N_PASS, H], U32, name="w_codes%d" % c, align_bytes=64) for c in range(2)]
+        w_scales = [sb.tile([P, N_PASS, H], U8, name="w_scales%d" % c, align_bytes=64) for c in range(2)]
+
+        x1_grouped = [sb.tile([P, 2, N_PASS, P, PACK], BF16, name="x1_grouped%d" % k, align_bytes=64)
+                      for k in range(N_PAIR)]
+        x1_codes = [sb.tile([P, 2, N_PASS, P], U32, name="x1_codes%d" % k, align_bytes=64) for k in range(N_PAIR)]
+        x1_scales = [sb.tile([P, 2, N_PASS, P], U8, name="x1_scales%d" % k, align_bytes=64) for k in range(N_PAIR)]
+        x2_grouped = [sb.tile([P, N_PASS, TILES_PER_HALF * P, PACK], BF16, name="x2_grouped%d" % g, align_bytes=64)
+                      for g in range(N_HALF)]
+        x2_codes = [sb.tile([P, N_PASS, TILES_PER_HALF * P], U32, name="x2_codes%d" % g, align_bytes=64)
+                    for g in range(N_HALF)]
+        x2_scales = [sb.tile([P, N_PASS, TILES_PER_HALF * P], U8, name="x2_scales%d" % g, align_bytes=64)
+                     for g in range(N_HALF)]
+
+        a_rows = [sb.tile([P, 2, H], F32, name="a_rows%d" % k) for k in range(N_PAIR)]
+        noisy_rows = [sb.tile([P, 2, H], F32, name="noisy_rows%d" % k) for k in range(N_PAIR)]
+        c_cols = [[sb.tile([P, TILES_PER_HALF * P], F32, name="c_cols%d_%d" % (g, t)) for t in range(N_CH)]
+                  for g in range(N_HALF)]
+        out_cols = [[sb.tile([P, TILES_PER_HALF * P], F32, name="out_cols%d_%d" % (g, t)) for t in range(N_CH)]
+                    for g in range(N_HALF)]
+        out_rows = [sb.tile([P, 2, H], F32, name="out_rows%d" % k) for k in range(N_PAIR)]
+        out_bytes = [sb.tile([P, 2, H], FP8, name="out_bytes%d" % k) for k in range(N_PAIR)]
+
+        def copy(engine, dst, src):
+            if engine == "vector":
+                nc.vector.tensor_copy(out=dst, in_=src)
+            else:
+                nc.scalar.copy(out=dst, in_=src)
+
+        def load_x(c, k):
+            src = (x1, x2)[c][2 * k * P:(2 * k + 2) * P, :]
+            nc.sync.dma_start(out=x_raw[c][k][:], in_=src.rearrange("(e p) f -> p e f", p=P))
+
+        def load_w(c, s):
+            src = (W1, W2)[c][s * K_PASS:(s + 1) * K_PASS, :]
+            nc.sync.dma_start(out=w_raw[c][s][:], in_=src.rearrange("(p j) h -> p j h", j=PACK))
+
+        def interleave_w(engine, c, s, col0, col1):
+            dst = w_grouped[c][:, s, col0:col1, :]
+            src = w_raw[c][s][:, :, col0:col1].rearrange("p j h -> p h j")
+            if engine == "gpsimd":
+                nc.gpsimd.tensor_scalar(out=dst, in0=src, scalar1=1.0, scalar2=0.0, op0=ALU.mult, op1=ALU.add)
+            else:
+                copy(engine, dst, src)
+
+        def quantize(codes, scales, grouped):
+            nc.vector.quantize_mx(out=codes.bitcast(FP8X4), scales=scales, in_=grouped)
+
+        def quantize_w1(s):
+            quantize(w_codes[0][:, s, :], w_scales[0][:, s, :], w_grouped[0][:, s, :, :].rearrange("p h j -> p (h j)"))
+
+        def quantize_w2():
+            quantize(w_codes[1][:].rearrange("p s h -> p (s h)"), w_scales[1][:].rearrange("p s h -> p (s h)"),
+                     w_grouped[1][:].rearrange("p s h j -> p (s h j)"))
+
+        def transpose_x(c, i):
+            bank = new_bank(("x", c, i), [P, 2 * N_PASS, P], F32)
+            words = x_raw[c][i // 2][:, i % 2, :].bitcast(F32)
+            half_pass = K_PASS // 2
+            for s in range(N_PASS):
+                for u in range(2):
+                    nc.tensor.transpose(bank[:, 2 * s + u, :], words[:, half_pass * s + u:half_pass * (s + 1):2],
+                                        ident_f32[:])
+
+        def group_x1(i):
+            copy("scalar", x1_grouped[i // 2][:, i % 2, :, :, :].bitcast(F32),
+                     banks[("x", 0, i)][:].rearrange("p (s u) r -> p s r u", u=2))
+
+        def group_x2(i):
+            g, q = divmod(i, TILES_PER_HALF)
+            copy("scalar", x2_grouped[g][:, :, q * P:(q + 1) * P, :].bitcast(F32),
+                     banks[("x", 1, i)][:].rearrange("p (s u) r -> p s r u", u=2))
+
+        def quantize_x1_tile(i):
+            k, e = divmod(i, 2)
+            quantize(x1_codes[k][:, e, :, :].rearrange("p s r -> p (s r)"),
+                     x1_scales[k][:, e, :, :].rearrange("p s r -> p (s r)"),
+                     x1_grouped[k][:, e, :, :, :].rearrange("p s r j -> p (s r j)"))
+
+        def quantize_x1_pair(k):
+            quantize(x1_codes[k][:].rearrange("p e s r -> p (e s r)"), x1_scales[k][:].rearrange("p e s r -> p (e s r)"),
+                     x1_grouped[k][:].rearrange("p e s r j -> p (e s r j)"))
+
+        def quantize_x2(g):
+            quantize(x2_codes[g][:].rearrange("p s r -> p (s r)"), x2_scales[g][:].rearrange("p s r -> p (s r)"),
+                     x2_grouped[g][:].rearrange("p s r j -> p (s r j)"))
+
+        def matmul_client1(i):
+            k, e = divmod(i, 2)
+            acc = new_bank(("p1", i), [P, H], F32)
+            for s in range(N_PASS):
+                nc.tensor.matmul_mx(out=acc[:], lhsT=x1_codes[k][:, e, s, :].bitcast(FP8X4),
+                                    lhsT_scale=x1_scales[k][:, e, s, :], rhs=w_codes[0][:, s, :].bitcast(FP8X4),
+                                    rhs_scale=w_scales[0][:, s, :], start=(s == 0), stop=(s == N_PASS - 1))
+
+        def matmul_client2(g, t):
+            acc = new_bank(("p2", g, t), [P, TILES_PER_HALF * P], F32)
+            channels = slice(t * P, (t + 1) * P)
+            for s in range(N_PASS):
+                nc.tensor.matmul_mx(out=acc[:], lhsT=w_codes[1][:, s, channels].bitcast(FP8X4),
+                                    lhsT_scale=w_scales[1][:, s, channels], rhs=x2_codes[g][:, s, :].bitcast(FP8X4),
+                                    rhs_scale=x2_scales[g][:, s, :], start=(s == 0), stop=(s == N_PASS - 1))
+
+        def add_b1(i):
+            nc.vector.tensor_tensor(out=a_rows[i // 2][:, i % 2, :], in0=banks[("p1", i)][:], in1=b1_all[:], op=ALU.add)
+
+        def row_norm(i):
+            absolute = scratch.tile([P, H], BF16, name="absolute")
+            nc.scalar.activation(out=absolute[:], in_=a_rows[i // 2][:, i % 2, :], func=ACT.Abs,
+                                 accum_out=norms[:, 0, i:i + 1])
+
+        def add_noise(k):
+            nc.vector.scalar_tensor_tensor(out=noisy_rows[k][:], in0=noise[:, 2 * k:2 * k + 2, :],
+                                           scalar=noise_mul[:, 0:1], in1=a_rows[k][:], op0=ALU.mult, op1=ALU.add)
+
+        def transpose_noisy(g, t):
+            bank = new_bank(("c", g, t), [P, TILES_PER_HALF * P], F32)
+            for q in range(TILES_PER_HALF):
+                i = TILES_PER_HALF * g + q
+                nc.tensor.transpose(bank[:, q * P:(q + 1) * P], noisy_rows[i // 2][:, i % 2, t * P:(t + 1) * P],
+                                    ident_f32[:])
+
+        def mask_c(g, t):
+            nc.scalar.activation(out=c_cols[g][t][:], in_=banks[("c", g, t)][:], func=ACT.Copy,
+                                 scale=keep_cols[:, t:t + 1])
+
+        def fuse(g, t):
+            nc.vector.scalar_tensor_tensor(out=out_cols[g][t][:], in0=banks[("p2", g, t)][:], scalar=vec_cols[:, t:t + 1],
+                                           in1=c_cols[g][t][:], op0=ALU.add, op1=ALU.min)
+
+        def transpose_out(i):
+            g, q = divmod(i, TILES_PER_HALF)
+            bank = new_bank(("out", i), [P, H], F32)
+            for t in range(N_CH):
+                nc.tensor.transpose(bank[:, t * P:(t + 1) * P], out_cols[g][t][:, q * P:(q + 1) * P], ident_f32[:])
+
+        def pair_rows(dram, k):
+            return dram[2 * k * P:(2 * k + 2) * P, :].rearrange("(e p) h -> p e h", p=P)
+
+        def bring_back(k):
+            for i in (2 * k, 2 * k + 1):
+                transpose_out(i)
+            for i in (2 * k, 2 * k + 1):
+                copy("scalar", out_rows[k][:, i % 2, :], banks[("out", i)][:])
+            nc.sync.dma_start(out=pair_rows(out_0, k), in_=out_rows[k][:])
+
+        def amax_pair(k):
+            nc.vector.tensor_reduce(out=row_amax[:, 2 * k:2 * k + 2], in_=out_rows[k][:], axis=AX.X, op=ALU.max,
+                                    apply_absolute_value=True)
+
+        def scale_of_rows(i0, i1):
+            nc.vector.reciprocal(out=row_rcp[:, i0:i1], in_=row_amax[:, i0:i1])
+            nc.scalar.activation(out=row_scale[:, i0:i1], in_=row_rcp[:, i0:i1], func=ACT.Copy, scale=FP8_MAX)
+
+        def cast(i):
+            dst = out_bytes[i // 2][:, i % 2, :]
+            src = out_rows[i // 2][:, i % 2, :]
+            if i in VECTOR_CASTS:
+                nc.vector.tensor_scalar(out=dst, in0=src, scalar1=row_scale[:, i:i + 1], scalar2=None, op0=ALU.mult,
+                                        saturate=False)
+            else:
+                nc.scalar.activation(out=dst, in_=src, func=ACT.Identity, scale=row_scale[:, i:i + 1],
+                                     bias=zero_col[:, 0:1], saturate=False)
+
+        def cast_pair(k):
+            cast(2 * k)
+            cast(2 * k + 1)
+            nc.sync.dma_start(out=pair_rows(out_1, k), in_=out_bytes[k][:].bitcast(U8))
+
+        nc.vector.memset(zero_col[:], 0.0)
+        nc.scalar.activation(out=act_warm[:], in_=zero_col[:], func=ACT.Abs)
+        nc.vector.memset(b1_row[:], 0.0)
+        nc.vector.memset(vec_rows[:], 0.0)
+        nc.vector.memset(ones[:], 1.0)
+        make_identity(nc, ident_f32[:])
+        make_identity(nc, ident_bf16[:])
+
+        load_w(0, 0)
+        load_w(0, 1)
+        load_x(0, 0)
+        nc.sync.dma_start(out=b1_row[0:1, :], in_=b1.rearrange("(o h) -> o h", o=1))
+        for k in range(1, N_PAIR):
+            load_x(0, k)
+        nc.sync.dma_start(out=vec_rows[0:N_CH, :], in_=b2.rearrange("(t p) -> t p", p=P))
+        nc.sync.dma_start(out=vec_rows[N_CH:2 * N_CH, :], in_=rr_uniform.rearrange("(t p) -> t p", p=P))
+        load_w(1, 0)
+        load_w(1, 1)
+        load_x(1, 0)
+        load_x(1, 1)
+        nc.sync.dma_start(out=noise[:], in_=noise_std.rearrange("(i p) h -> p i h", p=P))
+        load_x(1, 2)
+        load_x(1, 3)
+
+        for s in range(N_PASS):
+            for col0 in range(0, H, W2_PIECE_COLS):
+                interleave_w("gpsimd", 1, s, col0, col0 + W2_PIECE_COLS)
+
+        for s in range(N_PASS):
+            interleave_w("scalar", 0, s, W1_VECTOR_COLS, H)
+            interleave_w("vector", 0, s, 0, W1_VECTOR_COLS)
+        for s in range(N_PASS):
+            quantize_w1(s)
+
+        transpose_x(0, 0)
+        transpose_x(0, 1)
+        b1_bank = new_bank("b1", [P, H], F32)
+        nc.tensor.matmul(b1_bank[:], lhsT=ones[:], rhs=b1_row[:], start=True, stop=True)
+        group_x1(0)
+        group_x1(1)
+        transpose_x(0, 2)
+        transpose_x(0, 3)
+        quantize_x1_tile(0)
+        quantize_x1_tile(1)
+        copy("vector", b1_all[:], b1_bank[:])
+        group_x1(2)
+        group_x1(3)
+
+        for k in range(N_PAIR):
+            matmul_client1(2 * k)
+            matmul_client1(2 * k + 1)
+            if k + 2 < N_PAIR:
+                transpose_x(0, 2 * k + 4)
+                transpose_x(0, 2 * k + 5)
+            if k == N_PAIR - 2:
+                vec_bank = new_bank("vec", [P, P], BF16)
+                nc.tensor.transpose(vec_bank[:], vec_rows[:], ident_bf16[:])
+            if k + 1 < N_PAIR:
+                quantize_x1_pair(k + 1)
+            add_b1(2 * k)
+            add_b1(2 * k + 1)
+            if k + 2 < N_PAIR:
+                group_x1(2 * k + 4)
+                group_x1(2 * k + 5)
+            if k == N_PAIR - 2:
+                nc.scalar.copy(out=vec_cols[:], in_=vec_bank[:, 0:2 * N_CH])
+                nc.gpsimd.tensor_scalar(out=keep_cols[:], in0=vec_cols[:, N_CH:2 * N_CH], scalar1=P_KEEP, scalar2=None,
+                                        op0=ALU.is_lt)
+            row_norm(2 * k)
+            row_norm(2 * k + 1)
+
+        for i in range(TILES_PER_HALF):
+            transpose_x(1, i)
+        nc.scalar.activation(out=norms[:, 1, :], in_=norms[:, 0, :], func=ACT.Copy, scale=-1.0)
+        quantize_w2()
+        nc.vector.tensor_reduce(out=part_ext[:], in_=norms[:], axis=AX.X, op=ALU.max)
+        ext_bank = new_bank("ext", [P, 2, P], F32)
+        for j in range(2):
+            nc.tensor.transpose(ext_bank[:, j, :], part_ext[:, j:j + 1].to_broadcast([P, P]), ident_f32[:])
+        nc.vector.tensor_reduce(out=all_ext[:], in_=ext_bank[:], axis=AX.X, op=ALU.max)
+        nc.vector.tensor_scalar(out=noise_mul[:], in0=all_ext[:, 0:1], scalar1=all_ext[:, 1:2], scalar2=1.0 / EPS,
+                                op0=ALU.add, op1=ALU.mult)
+
+        for i in range(TILES_PER_HALF):
+            group_x2(i)
+        for i in range(TILES_PER_HALF, N_TILE):
+            transpose_x(1, i)
+            group_x2(i)
+
+        for g in range(N_HALF):
+            add_noise(2 * g)
+            add_noise(2 * g + 1)
+            if g > 0:
+                for t in range(N_CH):
+                    matmul_client2(g - 1, t)
+            for t in range(N_CH):
+                transpose_noisy(g, t)
+                mask_c(g, t)
+            quantize_x2(g)
+        for t in range(N_CH):
+            fuse(0, t)
+        for t in range(N_CH - 1):
+            matmul_client2(1, t)
+        bring_back(0)
+        matmul_client2(1, N_CH - 1)
+        fuse(1, 0)
+        fuse(1, 1)
+        bring_back(1)
+        fuse(1, 2)
+        fuse(1, 3)
+
+        amax_pair(0)
+        bring_back(2)
+        amax_pair(1)
+        bring_back(3)
+        scale_of_rows(0, 4)
+        amax_pair(2)
+        cast_pair(0)
+        cast_pair(1)
+        scale_of_rows(4, 6)
+        amax_pair(3)
+        cast_pair(2)
+        scale_of_rows(6, 8)
+        cast_pair(3)

@@ -254,17 +254,16 @@ def tile_splitnn_pa_kernel(tc, x1, x2, W1, b1, W2, b2, noise_std, rr_uniform, ou
         load_w(0, 1)
         load_x(0, 0)
         nc.sync.dma_start(out=b1_row[0:1, :], in_=b1.rearrange("(o h) -> o h", o=1))
-        for k in range(1, N_PAIR):
-            load_x(0, k)
+        load_x(0, 1)
+        load_x(0, 2)
+        load_w(1, 0)
+        load_x(0, 3)
+        load_w(1, 1)
         nc.sync.dma_start(out=vec_rows[0:N_CH, :], in_=b2.rearrange("(t p) -> t p", p=P))
         nc.sync.dma_start(out=vec_rows[N_CH:2 * N_CH, :], in_=rr_uniform.rearrange("(t p) -> t p", p=P))
-        load_w(1, 0)
-        load_w(1, 1)
-        load_x(1, 0)
-        load_x(1, 1)
+        for k in range(N_PAIR):
+            load_x(1, k)
         nc.sync.dma_start(out=noise[:], in_=noise_std.rearrange("(i p) h -> p i h", p=P))
-        load_x(1, 2)
-        load_x(1, 3)
 
         for s in range(N_PASS):
             for col0 in range(0, H, W2_PIECE_COLS):

from contextlib import ExitStack

import concourse.mybir as mybir
from concourse.masks import make_identity

F32 = mybir.dt.float32
BF16 = mybir.dt.bfloat16
U32 = mybir.dt.uint32
U8 = mybir.dt.uint8
FP8X4 = mybir.dt.float8_e4m3fn_x4
FP8 = mybir.dt.float8_e4m3fn
ALU = mybir.AluOpType
ACT = mybir.ActivationFunctionType
AX = mybir.AxisListType

B, F, H = 1024, 1024, 512
EPS = 4.0 / 30.0
P_KEEP = 0.95
FP8_MAX = 448.0
FLOPS = 2 * 2 * B * F * H

P = 128
PACK = 4
K_PASS = P * PACK
N_PASS = F // K_PASS
N_TILE = B // P
N_PAIR = N_TILE // 2
N_HALF = 2
TILES_PER_HALF = N_TILE // N_HALF
N_CH = H // P
PSUM_BANKS = 8

W1_VECTOR_COLS = 352
W2_PIECE_COLS = 128
VECTOR_CASTS = (3, 5, 7)


def tile_splitnn_pa_kernel(tc, x1, x2, W1, b1, W2, b2, noise_std, rr_uniform, out_0, out_1):
    nc = tc.nc

    with ExitStack() as ctx:
        sb = ctx.enter_context(tc.tile_pool(name="sb", bufs=1))
        scratch = ctx.enter_context(tc.tile_pool(name="scratch", bufs=2))
        ps = ctx.enter_context(tc.psum_pool(name="ps", bufs=PSUM_BANKS))
        ctx.enter_context(tc.manual_schedule())

        banks = {}

        def new_bank(key, shape, dtype):
            banks[key] = ps.tile(shape, dtype, name="bank")
            return banks[key]

        zero_col = sb.tile([P, 1], F32, name="zero_col")
        act_warm = sb.tile([P, 1], F32, name="act_warm")
        ones = sb.tile([P, P], BF16, name="ones")
        ident_f32 = sb.tile([P, P], F32, name="ident_f32")
        ident_bf16 = sb.tile([P, P], BF16, name="ident_bf16")
        b1_row = sb.tile([P, H], BF16, name="b1_row")
        vec_rows = sb.tile([P, P], BF16, name="vec_rows")
        b1_all = sb.tile([P, H], F32, name="b1_all")
        vec_cols = sb.tile([P, 2 * N_CH], F32, name="vec_cols")
        keep_cols = sb.tile([P, N_CH], F32, name="keep_cols")
        norms = sb.tile([P, 2, N_TILE], F32, name="norms")
        part_ext = sb.tile([P, 2], F32, name="part_ext")
        all_ext = sb.tile([P, 2], F32, name="all_ext")
        noise_mul = sb.tile([P, 1], F32, name="noise_mul")
        row_amax = sb.tile([P, N_TILE], F32, name="row_amax")
        row_rcp = sb.tile([P, N_TILE], F32, name="row_rcp")
        row_scale = sb.tile([P, N_TILE], F32, name="row_scale")

        x_raw = [[sb.tile([P, 2, F], BF16, name="x_raw%d_%d" % (c, k)) for k in range(N_PAIR)] for c in range(2)]
        w_raw = [[sb.tile([P, PACK, H], BF16, name="w_raw%d_%d" % (c, s)) for s in range(N_PASS)] for c in range(2)]
        noise = sb.tile([P, N_TILE, H], BF16, name="noise")

        w_grouped = [sb.tile([P, N_PASS, H, PACK], BF16, name="w_grouped%d" % c, align_bytes=64) for c in range(2)]
        w_codes = [sb.tile([P, N_PASS, H], U32, name="w_codes%d" % c, align_bytes=64) for c in range(2)]
        w_scales = [sb.tile([P, N_PASS, H], U8, name="w_scales%d" % c, align_bytes=64) for c in range(2)]

        x1_grouped = [sb.tile([P, 2, N_PASS, P, PACK], BF16, name="x1_grouped%d" % k, align_bytes=64)
                      for k in range(N_PAIR)]
        x1_codes = [sb.tile([P, 2, N_PASS, P], U32, name="x1_codes%d" % k, align_bytes=64) for k in range(N_PAIR)]
        x1_scales = [sb.tile([P, 2, N_PASS, P], U8, name="x1_scales%d" % k, align_bytes=64) for k in range(N_PAIR)]
        x2_grouped = [sb.tile([P, N_PASS, TILES_PER_HALF * P, PACK], BF16, name="x2_grouped%d" % g, align_bytes=64)
                      for g in range(N_HALF)]
        x2_codes = [sb.tile([P, N_PASS, TILES_PER_HALF * P], U32, name="x2_codes%d" % g, align_bytes=64)
                    for g in range(N_HALF)]
        x2_scales = [sb.tile([P, N_PASS, TILES_PER_HALF * P], U8, name="x2_scales%d" % g, align_bytes=64)
                     for g in range(N_HALF)]

        a_rows = [sb.tile([P, 2, H], F32, name="a_rows%d" % k) for k in range(N_PAIR)]
        noisy_rows = [sb.tile([P, 2, H], F32, name="noisy_rows%d" % k) for k in range(N_PAIR)]
        c_cols = [[sb.tile([P, TILES_PER_HALF * P], F32, name="c_cols%d_%d" % (g, t)) for t in range(N_CH)]
                  for g in range(N_HALF)]
        out_cols = [[sb.tile([P, TILES_PER_HALF * P], F32, name="out_cols%d_%d" % (g, t)) for t in range(N_CH)]
                    for g in range(N_HALF)]
        out_rows = [sb.tile([P, 2, H], F32, name="out_rows%d" % k) for k in range(N_PAIR)]
        out_bytes = [sb.tile([P, 2, H], FP8, name="out_bytes%d" % k) for k in range(N_PAIR)]

        def copy(engine, dst, src):
            if engine == "vector":
                nc.vector.tensor_copy(out=dst, in_=src)
            else:
                nc.scalar.copy(out=dst, in_=src)

        def load_x(c, k):
            src = (x1, x2)[c][2 * k * P:(2 * k + 2) * P, :]
            nc.sync.dma_start(out=x_raw[c][k][:], in_=src.rearrange("(e p) f -> p e f", p=P))

        def load_w(c, s):
            src = (W1, W2)[c][s * K_PASS:(s + 1) * K_PASS, :]
            nc.sync.dma_start(out=w_raw[c][s][:], in_=src.rearrange("(p j) h -> p j h", j=PACK))

        def interleave_w(engine, c, s, col0, col1):
            dst = w_grouped[c][:, s, col0:col1, :]
            src = w_raw[c][s][:, :, col0:col1].rearrange("p j h -> p h j")
            if engine == "gpsimd":
                nc.gpsimd.tensor_scalar(out=dst, in0=src, scalar1=1.0, scalar2=0.0, op0=ALU.mult, op1=ALU.add)
            else:
                copy(engine, dst, src)

        def quantize(codes, scales, grouped):
            nc.vector.quantize_mx(out=codes.bitcast(FP8X4), scales=scales, in_=grouped)

        def quantize_w1(s):
            quantize(w_codes[0][:, s, :], w_scales[0][:, s, :], w_grouped[0][:, s, :, :].rearrange("p h j -> p (h j)"))

        def quantize_w2():
            quantize(w_codes[1][:].rearrange("p s h -> p (s h)"), w_scales[1][:].rearrange("p s h -> p (s h)"),
                     w_grouped[1][:].rearrange("p s h j -> p (s h j)"))

        def transpose_x(c, i):
            bank = new_bank(("x", c, i), [P, 2 * N_PASS, P], F32)
            words = x_raw[c][i // 2][:, i % 2, :].bitcast(F32)
            half_pass = K_PASS // 2
            for s in range(N_PASS):
                for u in range(2):
                    nc.tensor.transpose(bank[:, 2 * s + u, :], words[:, half_pass * s + u:half_pass * (s + 1):2],
                                        ident_f32[:])

        def group_x1(i):
            copy("scalar", x1_grouped[i // 2][:, i % 2, :, :, :].bitcast(F32),
                     banks[("x", 0, i)][:].rearrange("p (s u) r -> p s r u", u=2))

        def group_x2(i):
            g, q = divmod(i, TILES_PER_HALF)
            copy("scalar", x2_grouped[g][:, :, q * P:(q + 1) * P, :].bitcast(F32),
                     banks[("x", 1, i)][:].rearrange("p (s u) r -> p s r u", u=2))

        def quantize_x1_tile(i):
            k, e = divmod(i, 2)
            quantize(x1_codes[k][:, e, :, :].rearrange("p s r -> p (s r)"),
                     x1_scales[k][:, e, :, :].rearrange("p s r -> p (s r)"),
                     x1_grouped[k][:, e, :, :, :].rearrange("p s r j -> p (s r j)"))

        def quantize_x1_pair(k):
            quantize(x1_codes[k][:].rearrange("p e s r -> p (e s r)"), x1_scales[k][:].rearrange("p e s r -> p (e s r)"),
                     x1_grouped[k][:].rearrange("p e s r j -> p (e s r j)"))

        def quantize_x2(g):
            quantize(x2_codes[g][:].rearrange("p s r -> p (s r)"), x2_scales[g][:].rearrange("p s r -> p (s r)"),
                     x2_grouped[g][:].rearrange("p s r j -> p (s r j)"))

        def matmul_client1(i):
            k, e = divmod(i, 2)
            acc = new_bank(("p1", i), [P, H], F32)
            for s in range(N_PASS):
                nc.tensor.matmul_mx(out=acc[:], lhsT=x1_codes[k][:, e, s, :].bitcast(FP8X4),
                                    lhsT_scale=x1_scales[k][:, e, s, :], rhs=w_codes[0][:, s, :].bitcast(FP8X4),
                                    rhs_scale=w_scales[0][:, s, :], start=(s == 0), stop=(s == N_PASS - 1))

        def matmul_client2(g, t):
            acc = new_bank(("p2", g, t), [P, TILES_PER_HALF * P], F32)
            channels = slice(t * P, (t + 1) * P)
            for s in range(N_PASS):
                nc.tensor.matmul_mx(out=acc[:], lhsT=w_codes[1][:, s, channels].bitcast(FP8X4),
                                    lhsT_scale=w_scales[1][:, s, channels], rhs=x2_codes[g][:, s, :].bitcast(FP8X4),
                                    rhs_scale=x2_scales[g][:, s, :], start=(s == 0), stop=(s == N_PASS - 1))

        def add_b1(i):
            nc.vector.tensor_tensor(out=a_rows[i // 2][:, i % 2, :], in0=banks[("p1", i)][:], in1=b1_all[:], op=ALU.add)

        def row_norm(i):
            absolute = scratch.tile([P, H], BF16, name="absolute")
            nc.scalar.activation(out=absolute[:], in_=a_rows[i // 2][:, i % 2, :], func=ACT.Abs,
                                 accum_out=norms[:, 0, i:i + 1])

        def add_noise(k):
            nc.vector.scalar_tensor_tensor(out=noisy_rows[k][:], in0=noise[:, 2 * k:2 * k + 2, :],
                                           scalar=noise_mul[:, 0:1], in1=a_rows[k][:], op0=ALU.mult, op1=ALU.add)

        def transpose_noisy(g, t):
            bank = new_bank(("c", g, t), [P, TILES_PER_HALF * P], F32)
            for q in range(TILES_PER_HALF):
                i = TILES_PER_HALF * g + q
                nc.tensor.transpose(bank[:, q * P:(q + 1) * P], noisy_rows[i // 2][:, i % 2, t * P:(t + 1) * P],
                                    ident_f32[:])

        def mask_c(g, t):
            nc.scalar.activation(out=c_cols[g][t][:], in_=banks[("c", g, t)][:], func=ACT.Copy,
                                 scale=keep_cols[:, t:t + 1])

        def fuse(g, t):
            nc.vector.scalar_tensor_tensor(out=out_cols[g][t][:], in0=banks[("p2", g, t)][:], scalar=vec_cols[:, t:t + 1],
                                           in1=c_cols[g][t][:], op0=ALU.add, op1=ALU.min)

        def transpose_out(i):
            g, q = divmod(i, TILES_PER_HALF)
            bank = new_bank(("out", i), [P, H], F32)
            for t in range(N_CH):
                nc.tensor.transpose(bank[:, t * P:(t + 1) * P], out_cols[g][t][:, q * P:(q + 1) * P], ident_f32[:])

        def pair_rows(dram, k):
            return dram[2 * k * P:(2 * k + 2) * P, :].rearrange("(e p) h -> p e h", p=P)

        def bring_back(k):
            for i in (2 * k, 2 * k + 1):
                transpose_out(i)
            for i in (2 * k, 2 * k + 1):
                copy("scalar", out_rows[k][:, i % 2, :], banks[("out", i)][:])
            nc.sync.dma_start(out=pair_rows(out_0, k), in_=out_rows[k][:])

        def amax_pair(k):
            nc.vector.tensor_reduce(out=row_amax[:, 2 * k:2 * k + 2], in_=out_rows[k][:], axis=AX.X, op=ALU.max,
                                    apply_absolute_value=True)

        def scale_of_rows(i0, i1):
            nc.vector.reciprocal(out=row_rcp[:, i0:i1], in_=row_amax[:, i0:i1])
            nc.scalar.activation(out=row_scale[:, i0:i1], in_=row_rcp[:, i0:i1], func=ACT.Copy, scale=FP8_MAX)

        def cast(i):
            dst = out_bytes[i // 2][:, i % 2, :]
            src = out_rows[i // 2][:, i % 2, :]
            if i in VECTOR_CASTS:
                nc.vector.tensor_scalar(out=dst, in0=src, scalar1=row_scale[:, i:i + 1], scalar2=None, op0=ALU.mult,
                                        saturate=False)
            else:
                nc.scalar.activation(out=dst, in_=src, func=ACT.Identity, scale=row_scale[:, i:i + 1],
                                     bias=zero_col[:, 0:1], saturate=False)

        def cast_pair(k):
            cast(2 * k)
            cast(2 * k + 1)
            nc.sync.dma_start(out=pair_rows(out_1, k), in_=out_bytes[k][:].bitcast(U8))

        nc.vector.memset(zero_col[:], 0.0)
        nc.scalar.activation(out=act_warm[:], in_=zero_col[:], func=ACT.Abs)
        nc.vector.memset(b1_row[:], 0.0)
        nc.vector.memset(vec_rows[:], 0.0)
        nc.vector.memset(ones[:], 1.0)
        make_identity(nc, ident_f32[:])
        make_identity(nc, ident_bf16[:])

        load_w(0, 0)
        load_w(0, 1)
        load_x(0, 0)
        nc.sync.dma_start(out=b1_row[0:1, :], in_=b1.rearrange("(o h) -> o h", o=1))
        load_x(0, 1)
        load_x(0, 2)
        load_w(1, 0)
        load_x(0, 3)
        load_w(1, 1)
        nc.sync.dma_start(out=vec_rows[0:N_CH, :], in_=b2.rearrange("(t p) -> t p", p=P))
        nc.sync.dma_start(out=vec_rows[N_CH:2 * N_CH, :], in_=rr_uniform.rearrange("(t p) -> t p", p=P))
        for k in range(N_PAIR):
            load_x(1, k)
        nc.sync.dma_start(out=noise[:], in_=noise_std.rearrange("(i p) h -> p i h", p=P))

        for s in range(N_PASS):
            for col0 in range(0, H, W2_PIECE_COLS):
                interleave_w("gpsimd", 1, s, col0, col0 + W2_PIECE_COLS)

        for s in range(N_PASS):
            interleave_w("scalar", 0, s, W1_VECTOR_COLS, H)
            interleave_w("vector", 0, s, 0, W1_VECTOR_COLS)
        for s in range(N_PASS):
            quantize_w1(s)

        transpose_x(0, 0)
        transpose_x(0, 1)
        b1_bank = new_bank("b1", [P, H], F32)
        nc.tensor.matmul(b1_bank[:], lhsT=ones[:], rhs=b1_row[:], start=True, stop=True)
        group_x1(0)
        group_x1(1)
        transpose_x(0, 2)
        transpose_x(0, 3)
        quantize_x1_tile(0)
        quantize_x1_tile(1)
        copy("vector", b1_all[:], b1_bank[:])
        group_x1(2)
        group_x1(3)

        for k in range(N_PAIR):
            matmul_client1(2 * k)
            matmul_client1(2 * k + 1)
            if k + 2 < N_PAIR:
                transpose_x(0, 2 * k + 4)
                transpose_x(0, 2 * k + 5)
            if k == N_PAIR - 2:
                vec_bank = new_bank("vec", [P, P], BF16)
                nc.tensor.transpose(vec_bank[:], vec_rows[:], ident_bf16[:])
            if k + 1 < N_PAIR:
                quantize_x1_pair(k + 1)
            add_b1(2 * k)
            add_b1(2 * k + 1)
            if k + 2 < N_PAIR:
                group_x1(2 * k + 4)
                group_x1(2 * k + 5)
            if k == N_PAIR - 2:
                nc.scalar.copy(out=vec_cols[:], in_=vec_bank[:, 0:2 * N_CH])
                nc.gpsimd.tensor_scalar(out=keep_cols[:], in0=vec_cols[:, N_CH:2 * N_CH], scalar1=P_KEEP, scalar2=None,
                                        op0=ALU.is_lt)
            row_norm(2 * k)
            row_norm(2 * k + 1)

        for i in range(TILES_PER_HALF):
            transpose_x(1, i)
        nc.scalar.activation(out=norms[:, 1, :], in_=norms[:, 0, :], func=ACT.Copy, scale=-1.0)
        quantize_w2()
        nc.vector.tensor_reduce(out=part_ext[:], in_=norms[:], axis=AX.X, op=ALU.max)
        ext_bank = new_bank("ext", [P, 2, P], F32)
        for j in range(2):
            nc.tensor.transpose(ext_bank[:, j, :], part_ext[:, j:j + 1].to_broadcast([P, P]), ident_f32[:])
        nc.vector.tensor_reduce(out=all_ext[:], in_=ext_bank[:], axis=AX.X, op=ALU.max)
        nc.vector.tensor_scalar(out=noise_mul[:], in0=all_ext[:, 0:1], scalar1=all_ext[:, 1:2], scalar2=1.0 / EPS,
                                op0=ALU.add, op1=ALU.mult)

        for i in range(TILES_PER_HALF):
            group_x2(i)
        for i in range(TILES_PER_HALF, N_TILE):
            transpose_x(1, i)
            group_x2(i)

        for g in range(N_HALF):
            add_noise(2 * g)
            add_noise(2 * g + 1)
            if g > 0:
                for t in range(N_CH):
                    matmul_client2(g - 1, t)
            for t in range(N_CH):
                transpose_noisy(g, t)
                mask_c(g, t)
            quantize_x2(g)
        for t in range(N_CH):
            fuse(0, t)
        for t in range(N_CH - 1):
            matmul_client2(1, t)
        bring_back(0)
        matmul_client2(1, N_CH - 1)
        fuse(1, 0)
        fuse(1, 1)
        bring_back(1)
        fuse(1, 2)
        fuse(1, 3)

        amax_pair(0)
        bring_back(2)
        amax_pair(1)
        bring_back(3)
        scale_of_rows(0, 4)
        amax_pair(2)
        cast_pair(0)
        cast_pair(1)
        scale_of_rows(4, 6)
        amax_pair(3)
        cast_pair(2)
        scale_of_rows(6, 8)
        cast_pair(3)
